import numpy as np
import ml_dtypes


def mxq(x, axis, fmt="e4m3"):
    dtype, down = {"e4m3": (ml_dtypes.float8_e4m3fn, 7), "e5m2": (ml_dtypes.float8_e5m2, 14)}[fmt]
    v = np.moveaxis(np.asarray(x, np.float32).astype(ml_dtypes.bfloat16).astype(np.float64), axis, -1)
    blocks = v.reshape(v.shape[:-1] + (-1, 32))
    amax = np.abs(blocks).max(-1, keepdims=True)
    byte = np.maximum(np.where(amax > 0, np.frexp(amax)[1] - 1 + 127, 0) - down, 1)
    scale = np.exp2(byte - 127.0)
    codes = (blocks / scale).astype(np.float32).astype(dtype).astype(np.float64)
    return np.moveaxis((codes * scale).reshape(v.shape), -1, axis)


WIDE = False


def mx_kscale(k):
    if not WIDE:
        return np.ones(k)
    levels = np.array([10, -10, 5, -5, 0])
    a = np.random.permutation(np.resize(levels, k // 512 * 4)).reshape(k // 512, 4)
    idx = np.arange(k)
    return np.exp2(a[idx // 512, idx % 128 // 32])


BF16 = ml_dtypes.bfloat16


def bf(x):
    return np.asarray(x, np.float32).astype(BF16)


def f64(x):
    return np.asarray(x).astype(np.float64)


BQ, BK, L, H, DH = 4, 4, 512, 4, 128
D = H * DH


def setup_inputs():
    s, t = mx_kscale(D), mx_kscale(D)
    amp_q = 0.5 + np.random.random((BQ, 1, 1))
    amp_k = 0.5 + np.random.random((BK, 1, 1))
    return {
        "query_states": bf(np.random.standard_normal((BQ, L, D)) * amp_q * s),
        "key_states": bf(np.random.standard_normal((BK, L, D)) * amp_k * s),
        "Wq": bf(np.random.standard_normal((D, D)) * 0.8 / np.sqrt(D) * t[:, None] / s[None, :]),
        "bq": bf(np.random.standard_normal(D) * 0.3 * t),
        "Wk": bf(np.random.standard_normal((D, D)) * 0.8 / np.sqrt(D) / t[:, None] / s[None, :]),
        "bk": bf(np.random.standard_normal(D) * 0.3 / t),
        "logit_scale": bf(-1.5 + 0.1 * np.random.standard_normal(1)),
    }


def reference(query_states, key_states, Wq, bq, Wk, bk, logit_scale):
    q = (mxq(f64(query_states).reshape(BQ * L, D), 1, "e4m3") @ mxq(f64(Wq), 1, "e4m3").T) + f64(bq)
    k = (mxq(f64(key_states).reshape(BK * L, D), 1, "e4m3") @ mxq(f64(Wk), 1, "e4m3").T) + f64(bk)
    retrieve = mxq(q, 1, "e4m3") @ mxq(k, 1, "e4m3").T
    retrieve = retrieve.reshape(BQ, L, BK, L).transpose(0, 2, 1, 3)
    t2v = retrieve.max(axis=-1).sum(axis=2) / L
    v2t = retrieve.max(axis=-2).sum(axis=2) / L
    return np.exp(f64(logit_scale)) * (t2v + v2t) / 2.0

@@ -1,0 +1,250 @@
+from contextlib import ExitStack
+
+import concourse.mybir as mybir
+from concourse.masks import make_identity
+
+F32 = mybir.dt.float32
+BF16 = mybir.dt.bfloat16
+U32 = mybir.dt.uint32
+U8 = mybir.dt.uint8
+FP8X4 = mybir.dt.float8_e4m3fn_x4
+ACT = mybir.ActivationFunctionType
+ALU = mybir.AluOpType
+AXIS = mybir.AxisListType
+
+P = 128
+PACK = 4
+SAMPLES = 4
+ROWS = 512
+FEATURES = 512
+BLOCKS = ROWS // P
+WORDS = FEATURES // 2
+PAIRS = SAMPLES * SAMPLES
+MAXIMA = 2 * BLOCKS
+STORE_RUN = 8
+
+LOOKAHEAD = 4
+REST_AFTER_FLIP = 3
+REST_AFTER_PACK = 4
+
+FLOPS = 2 * (2 * SAMPLES * ROWS) * FEATURES * FEATURES + 2 * (SAMPLES * ROWS) ** 2 * FEATURES
+
+
+def tile_attention_pa_kernel(
+    tc, query_states, key_states, Wq, bq, Wk, bk, logit_scale, out
+):
+    nc = tc.nc
+    with ExitStack() as ctx:
+        ctx.enter_context(tc.manual_schedule())
+        keep = ctx.enter_context(tc.tile_pool(name="keep", bufs=1))
+        stage = ctx.enter_context(tc.tile_pool(name="stage", bufs=3))
+        banks = ctx.enter_context(tc.psum_pool(name="banks", bufs=8))
+
+        log_gain = keep.tile([P, 1], BF16, name="log_gain")
+        nc.scalar.dma_start(out=log_gain[:], in_=logit_scale.partition_broadcast(P))
+
+        def load_bias(vector, name):
+            narrow = keep.tile([P, PACK], BF16, name=name)
+            nc.scalar.dma_start(out=narrow[:], in_=vector.rearrange("(p t) -> p t", t=PACK))
+            return narrow
+
+        def load_rows(rows, name):
+            raw = keep.tile([P, BLOCKS * FEATURES], BF16, name=name + "_raw")
+            nc.sync.dma_start(out=raw[:], in_=rows.rearrange("(p r) f -> p (r f)", r=BLOCKS))
+            return {"name": name, "raw": raw}
+
+        bq_bf16 = load_bias(bq, "bq_bf16")
+        bk_bf16 = load_bias(bk, "bk_bf16")
+        wq = load_rows(Wq, "wq")
+        wk = load_rows(Wk, "wk")
+        q = []
+        k = []
+        for s in range(SAMPLES):
+            q.append(load_rows(query_states[s], "q%d" % s))
+            k.append(load_rows(key_states[s], "k%d" % s))
+
+        identity = keep.tile([P, P], F32, name="identity")
+        make_identity(nc, identity[:])
+        ones = keep.tile([P, P], F32, name="ones")
+        nc.vector.memset(ones[:], 1.0)
+        gain = keep.tile([P, 1], F32, name="gain")
+        nc.scalar.activation(out=gain[:], in_=log_gain[:], func=ACT.Exp)
+        bq_f32 = keep.tile([P, PACK], F32, name="bq_f32")
+        nc.vector.tensor_copy(out=bq_f32[:], in_=bq_bf16[:])
+        bk_f32 = keep.tile([P, PACK], F32, name="bk_f32")
+        nc.vector.tensor_copy(out=bk_f32[:], in_=bk_bf16[:])
+        for s in range(SAMPLES):
+            q[s]["weight"] = wq
+            q[s]["bias"] = bq_f32
+            k[s]["weight"] = wk
+            k[s]["bias"] = bk_f32
+        maxima = keep.tile([P, PAIRS * MAXIMA], F32, name="maxima")
+
+        def quantise(values, name):
+            codes = keep.tile([P, ROWS], U32, name=name + "_codes", align_bytes=64)
+            scales = keep.tile([P, ROWS], U8, name=name + "_scales", align_bytes=64)
+            nc.vector.quantize_mx(out=codes[:].bitcast(FP8X4), scales=scales[:], in_=values)
+            return codes, scales
+
+        def flip_rows(rows, half, on_vector):
+            if half == 0:
+                rows["grouped"] = stage.tile([P, ROWS * PACK], BF16, name="grouped", align_bytes=64)
+            words = rows["raw"][:].bitcast(F32)
+            flipped = banks.tile([P, 2, 2 * P], F32, name="flipped", tag="bank")
+            for r in range(2):
+                first_word = (2 * half + r) * WORDS
+                for u in range(2):
+                    nc.tensor.transpose(
+                        flipped[:, u, r * P : (r + 1) * P],
+                        words[:, first_word + u * P : first_word + (u + 1) * P],
+                        identity[:],
+                    )
+            grouped_words = rows["grouped"][:].bitcast(F32).rearrange("p (c u) -> p c u", u=2)
+            target = grouped_words[:, half * 2 * P : (half + 1) * 2 * P, :]
+            source = flipped[:].rearrange("p u c -> p c u")
+            if on_vector:
+                nc.vector.tensor_copy(out=target, in_=source)
+            else:
+                nc.scalar.copy(out=target, in_=source)
+
+        def quantise_rows(rows):
+            rows["rows_mx"] = quantise(rows["grouped"][:], "x" + rows["name"])
+
+        def project_plane(sample, t, on_vector):
+            if t == 0:
+                sample["planes"] = stage.tile([P, PACK, ROWS], BF16, name="planes")
+            w_codes, w_scales = sample["weight"]["rows_mx"]
+            x_codes, x_scales = sample["rows_mx"]
+            cols = slice(t * P, (t + 1) * P)
+            acc = banks.tile([P, ROWS], F32, name="acc", tag="bank")
+            nc.tensor.matmul_mx(
+                out=acc[:],
+                lhsT=w_codes[:, cols].bitcast(FP8X4),
+                lhsT_scale=w_scales[:, cols],
+                rhs=x_codes[:].bitcast(FP8X4),
+                rhs_scale=x_scales[:],
+                start=True,
+                stop=True,
+            )
+            plane = sample["planes"][:, t, :]
+            bias = sample["bias"][:, t : t + 1]
+            if on_vector:
+                nc.vector.tensor_scalar(out=plane, in0=acc[:], scalar1=bias, scalar2=None, op0=ALU.add)
+            else:
+                nc.scalar.activation(out=plane, in_=acc[:], func=ACT.Identity, bias=bias, scale=1.0)
+
+        def pack_features(sample, on_vector):
+            sample["packed"] = stage.tile([P, ROWS, PACK], BF16, name="packed", align_bytes=64)
+            target = sample["packed"][:].rearrange("p (c i) t -> p c t i", i=4)
+            source = sample["planes"][:].rearrange("p t (c i) -> p c t i", i=4)
+            if on_vector:
+                nc.vector.tensor_copy(out=target, in_=source)
+            else:
+                nc.scalar.copy(out=target, in_=source)
+
+        def quantise_features(sample):
+            sample["mx"] = quantise(
+                sample["packed"][:].rearrange("p c t -> p (c t)"), sample["name"]
+            )
+
+        for rows in (wq, wk, q[0], k[0]):
+            flip_rows(rows, 0, False)
+            flip_rows(rows, 1, True)
+            quantise_rows(rows)
+        for sample in (q[0], k[0]):
+            for t in range(PACK):
+                project_plane(sample, t, t % 2 == 1)
+        for sample in (q[1], k[1]):
+            flip_rows(sample, 0, False)
+            flip_rows(sample, 1, False)
+        for sample in (q[0], k[0]):
+            pack_features(sample, True)
+        for sample in (q[0], k[0]):
+            quantise_features(sample)
+        for sample in (q[1], k[1]):
+            quantise_rows(sample)
+
+        def rows_steps(sample):
+            return (
+                [None] * REST_AFTER_PACK
+                + [lambda: flip_rows(sample, 0, False), lambda: flip_rows(sample, 1, False)]
+                + [None] * REST_AFTER_FLIP
+                + [lambda: quantise_rows(sample), None]
+            )
+
+        def projection_steps(sample):
+            planes = [lambda t=t: project_plane(sample, t, False) for t in range(PACK)]
+            return planes + [lambda: pack_features(sample, False)]
+
+        steps = projection_steps(q[1]) + projection_steps(k[1])
+        for s in range(2, SAMPLES):
+            for sample in (q[s], k[s]):
+                steps.extend(rows_steps(sample) + projection_steps(sample))
+
+        pair_order = []
+        for s in range(SAMPLES):
+            pair_order.extend((a, s) for a in range(s + 1))
+            if s + 1 < SAMPLES:
+                pair_order.extend((s + 1, b) for b in range(s + 1))
+
+        waiting = []
+
+        def take_maximum():
+            logits, column = waiting.pop(0)
+            nc.vector.tensor_reduce(
+                out=maxima[:, column : column + 1], in_=logits[:], axis=AXIS.X, op=ALU.max
+            )
+
+        for a, b in pair_order:
+            for sample in (q[a], k[b]):
+                if "mx" not in sample:
+                    while len(waiting) > 1:
+                        take_maximum()
+                    quantise_features(sample)
+            for side, (stationary, moving) in enumerate(((q[a], k[b]), (k[b], q[a]))):
+                s_codes, s_scales = stationary["mx"]
+                m_codes, m_scales = moving["mx"]
+                for block in range(BLOCKS):
+                    cols = slice(block * P, (block + 1) * P)
+                    logits = banks.tile([P, ROWS], F32, name="logits", tag="bank")
+                    nc.tensor.matmul_mx(
+                        out=logits[:],
+                        lhsT=s_codes[:, cols].bitcast(FP8X4),
+                        lhsT_scale=s_scales[:, cols],
+                        rhs=m_codes[:].bitcast(FP8X4),
+                        rhs_scale=m_scales[:],
+                        start=True,
+                        stop=True,
+                    )
+                    waiting.append((logits, (a * SAMPLES + b) * MAXIMA + side * BLOCKS + block))
+                    if steps:
+                        step = steps.pop(0)
+                        if step is not None:
+                            step()
+                    if len(waiting) > LOOKAHEAD:
+                        take_maximum()
+        while waiting:
+            take_maximum()
+
+        sums = keep.tile([P, PAIRS], F32, name="sums")
+        nc.vector.tensor_reduce(
+            out=sums[:],
+            in_=maxima[:].rearrange("p (n c) -> p n c", c=MAXIMA),
+            axis=AXIS.X,
+            op=ALU.add,
+        )
+        totals = banks.tile([P, PAIRS], F32, name="totals", tag="bank")
+        nc.tensor.matmul(out=totals[:], lhsT=ones[:], rhs=sums[:], start=True, stop=True)
+        result = keep.tile([P, PAIRS // STORE_RUN, 2 * STORE_RUN], F32, name="result")
+        nc.vector.tensor_scalar(
+            out=result[:, :, 0:STORE_RUN],
+            in0=totals[:].rearrange("p (h c) -> p h c", c=STORE_RUN),
+            scalar1=gain[:, 0:1],
+            scalar2=1.0 / (2 * ROWS),
+            op0=ALU.mult,
+            op1=ALU.mult,
+        )
+        nc.sync.dma_start(
+            out=out.rearrange("(o h a) b -> o h (a b)", o=1, h=PAIRS // STORE_RUN),
+            in_=result[0:1, :, 0:STORE_RUN],
+        )

@@ -173,8 +173,8 @@ def tile_attention_pa_kernel(
             )
 
         def projection_steps(sample):
-            planes = [lambda t=t: project_plane(sample, t, False) for t in range(PACK)]
-            return planes + [lambda: pack_features(sample, False)]
+            passes = [lambda t=t: project_plane(sample, t, False) for t in range(PACK)]
+            return passes + [lambda: pack_features(sample, False)]
 
         steps = projection_steps(q[1]) + projection_steps(k[1])
         for s in range(2, SAMPLES):
@@ -198,7 +198,7 @@ def tile_attention_pa_kernel(
         for a, b in pair_order:
             for sample in (q[a], k[b]):
                 if "mx" not in sample:
-                    while len(waiting) > 1:
+                    while sample in (q[1], k[1]) and len(waiting) > 1:
                         take_maximum()
                     quantise_features(sample)
             for side, (stationary, moving) in enumerate(((q[a], k[b]), (k[b], q[a]))):

@@ -19,13 +19,16 @@ ROWS = 512
 FEATURES = 512
 BLOCKS = ROWS // P
 WORDS = FEATURES // 2
+PLANES = WORDS // P
+HALF = ROWS // 2
 PAIRS = SAMPLES * SAMPLES
 MAXIMA = 2 * BLOCKS
 STORE_RUN = 8
+TOKEN_RUN = 4
 
-LOOKAHEAD = 4
-REST_AFTER_FLIP = 3
-REST_AFTER_PACK = 4
+PSUM_BANKS = 8
+LOOKAHEAD = PSUM_BANKS // 2
+FOLD_LAG = 2
 
 FLOPS = 2 * (2 * SAMPLES * ROWS) * FEATURES * FEATURES + 2 * (SAMPLES * ROWS) ** 2 * FEATURES
 
@@ -38,7 +41,8 @@ def tile_attention_pa_kernel(
         ctx.enter_context(tc.manual_schedule())
         keep = ctx.enter_context(tc.tile_pool(name="keep", bufs=1))
         stage = ctx.enter_context(tc.tile_pool(name="stage", bufs=3))
-        banks = ctx.enter_context(tc.psum_pool(name="banks", bufs=8))
+        folds = ctx.enter_context(tc.tile_pool(name="folds", bufs=FOLD_LAG + 2))
+        banks = ctx.enter_context(tc.psum_pool(name="banks", bufs=PSUM_BANKS))
 
         log_gain = keep.tile([P, 1], BF16, name="log_gain")
         nc.scalar.dma_start(out=log_gain[:], in_=logit_scale.partition_broadcast(P))
@@ -48,20 +52,20 @@ def tile_attention_pa_kernel(
             nc.scalar.dma_start(out=narrow[:], in_=vector.rearrange("(p t) -> p t", t=PACK))
             return narrow
 
-        def load_rows(rows, name):
+        def load_matrix(matrix, name):
             raw = keep.tile([P, BLOCKS * FEATURES], BF16, name=name + "_raw")
-            nc.sync.dma_start(out=raw[:], in_=rows.rearrange("(p r) f -> p (r f)", r=BLOCKS))
+            nc.sync.dma_start(out=raw[:], in_=matrix.rearrange("(p r) f -> p (r f)", r=BLOCKS))
             return {"name": name, "raw": raw}
 
         bq_bf16 = load_bias(bq, "bq_bf16")
         bk_bf16 = load_bias(bk, "bk_bf16")
-        wq = load_rows(Wq, "wq")
-        wk = load_rows(Wk, "wk")
+        wq = load_matrix(Wq, "wq")
+        wk = load_matrix(Wk, "wk")
         q = []
         k = []
         for s in range(SAMPLES):
-            q.append(load_rows(query_states[s], "q%d" % s))
-            k.append(load_rows(key_states[s], "k%d" % s))
+            q.append(load_matrix(query_states[s], "q%d" % s))
+            k.append(load_matrix(key_states[s], "k%d" % s))
 
         identity = keep.tile([P, P], F32, name="identity")
         make_identity(nc, identity[:])
@@ -80,114 +84,96 @@ def tile_attention_pa_kernel(
             k[s]["bias"] = bk_f32
         maxima = keep.tile([P, PAIRS * MAXIMA], F32, name="maxima")
 
-        def quantise(values, name):
-            codes = keep.tile([P, ROWS], U32, name=name + "_codes", align_bytes=64)
-            scales = keep.tile([P, ROWS], U8, name=name + "_scales", align_bytes=64)
+        def quantise(values, columns, name):
+            codes = keep.tile([P, columns], U32, name=name + "_codes", align_bytes=64)
+            scales = keep.tile([P, columns], U8, name=name + "_scales", align_bytes=64)
             nc.vector.quantize_mx(out=codes[:].bitcast(FP8X4), scales=scales[:], in_=values)
             return codes, scales
 
-        def flip_rows(rows, half, on_vector):
-            if half == 0:
-                rows["grouped"] = stage.tile([P, ROWS * PACK], BF16, name="grouped", align_bytes=64)
-            words = rows["raw"][:].bitcast(F32)
-            flipped = banks.tile([P, 2, 2 * P], F32, name="flipped", tag="bank")
-            for r in range(2):
-                first_word = (2 * half + r) * WORDS
-                for u in range(2):
-                    nc.tensor.transpose(
-                        flipped[:, u, r * P : (r + 1) * P],
-                        words[:, first_word + u * P : first_word + (u + 1) * P],
-                        identity[:],
-                    )
-            grouped_words = rows["grouped"][:].bitcast(F32).rearrange("p (c u) -> p c u", u=2)
-            target = grouped_words[:, half * 2 * P : (half + 1) * 2 * P, :]
-            source = flipped[:].rearrange("p u c -> p c u")
-            if on_vector:
-                nc.vector.tensor_copy(out=target, in_=source)
-            else:
-                nc.scalar.copy(out=target, in_=source)
+        def flip_rows(mat):
+            mat["grouped"] = stage.tile([P, ROWS * PACK], BF16, name="grouped", align_bytes=64)
+            words = mat["raw"][:].bitcast(F32)
+            grouped_words = mat["grouped"][:].bitcast(F32).rearrange("p (c u) -> p c u", u=PLANES)
+            for half in range(ROWS // HALF):
+                flipped = banks.tile([P, PLANES, HALF], F32, name="flipped", tag="bank")
+                for r in range(HALF // P):
+                    first_word = (half * (HALF // P) + r) * WORDS
+                    for u in range(PLANES):
+                        nc.tensor.transpose(
+                            flipped[:, u, r * P : (r + 1) * P],
+                            words[:, first_word + u * P : first_word + (u + 1) * P],
+                            identity[:],
+                        )
+                nc.scalar.copy(
+                    out=grouped_words[:, half * HALF : (half + 1) * HALF, :],
+                    in_=flipped[:].rearrange("p u c -> p c u"),
+                )
 
-        def quantise_rows(rows):
-            rows["rows_mx"] = quantise(rows["grouped"][:], "x" + rows["name"])
+        def quantise_rows(mat):
+            mat["rows_mx"] = quantise(mat["grouped"][:], ROWS, "x" + mat["name"])
 
-        def project_plane(sample, t, on_vector):
-            if t == 0:
-                sample["planes"] = stage.tile([P, PACK, ROWS], BF16, name="planes")
+        def project(sample, last_on_vector):
+            sample["planes"] = stage.tile([P, PACK, ROWS], BF16, name="planes")
             w_codes, w_scales = sample["weight"]["rows_mx"]
             x_codes, x_scales = sample["rows_mx"]
-            cols = slice(t * P, (t + 1) * P)
-            acc = banks.tile([P, ROWS], F32, name="acc", tag="bank")
-            nc.tensor.matmul_mx(
-                out=acc[:],
-                lhsT=w_codes[:, cols].bitcast(FP8X4),
-                lhsT_scale=w_scales[:, cols],
-                rhs=x_codes[:].bitcast(FP8X4),
-                rhs_scale=x_scales[:],
-                start=True,
-                stop=True,
-            )
-            plane = sample["planes"][:, t, :]
-            bias = sample["bias"][:, t : t + 1]
-            if on_vector:
-                nc.vector.tensor_scalar(out=plane, in0=acc[:], scalar1=bias, scalar2=None, op0=ALU.add)
-            else:
-                nc.scalar.activation(out=plane, in_=acc[:], func=ACT.Identity, bias=bias, scale=1.0)
-
-        def pack_features(sample, on_vector):
-            sample["packed"] = stage.tile([P, ROWS, PACK], BF16, name="packed", align_bytes=64)
-            target = sample["packed"][:].rearrange("p (c i) t -> p c t i", i=4)
-            source = sample["planes"][:].rearrange("p t (c i) -> p c t i", i=4)
-            if on_vector:
-                nc.vector.tensor_copy(out=target, in_=source)
-            else:
-                nc.scalar.copy(out=target, in_=source)
-
-        def quantise_features(sample):
-            sample["mx"] = quantise(
-                sample["packed"][:].rearrange("p c t -> p (c t)"), sample["name"]
-            )
-
-        for rows in (wq, wk, q[0], k[0]):
-            flip_rows(rows, 0, False)
-            flip_rows(rows, 1, True)
-            quantise_rows(rows)
-        for sample in (q[0], k[0]):
             for t in range(PACK):
-                project_plane(sample, t, t % 2 == 1)
-        for sample in (q[1], k[1]):
-            flip_rows(sample, 0, False)
-            flip_rows(sample, 1, False)
-        for sample in (q[0], k[0]):
-            pack_features(sample, True)
-        for sample in (q[0], k[0]):
-            quantise_features(sample)
-        for sample in (q[1], k[1]):
-            quantise_rows(sample)
+                cols = slice(t * P, (t + 1) * P)
+                acc = banks.tile([P, ROWS], F32, name="acc", tag="bank")
+                nc.tensor.matmul_mx(
+                    out=acc[:],
+                    lhsT=w_codes[:, cols].bitcast(FP8X4),
+                    lhsT_scale=w_scales[:, cols],
+                    rhs=x_codes[:].bitcast(FP8X4),
+                    rhs_scale=x_scales[:],
+                    start=True,
+                    stop=True,
+                )
+                plane = sample["planes"][:, t, :]
+                bias = sample["bias"][:, t : t + 1]
+                if last_on_vector and t == PACK - 1:
+                    nc.vector.tensor_scalar(
+                        out=plane, in0=acc[:], scalar1=bias, scalar2=None, op0=ALU.add
+                    )
+                else:
+                    nc.scalar.activation(
+                        out=plane, in_=acc[:], func=ACT.Identity, bias=bias, scale=1.0
+                    )
 
-        def rows_steps(sample):
-            return (
-                [None] * REST_AFTER_PACK
-                + [lambda: flip_rows(sample, 0, False), lambda: flip_rows(sample, 1, False)]
-                + [None] * REST_AFTER_FLIP
-                + [lambda: quantise_rows(sample), None]
+        def quantise_features(sample, with_negative):
+            packed = stage.tile([P, ROWS * PACK], BF16, name="packed", align_bytes=64)
+            nc.vector.tensor_copy(
+                out=packed[:].rearrange("p (c i t) -> p c t i", i=TOKEN_RUN, t=PACK),
+                in_=sample["planes"][:].rearrange("p t (c i) -> p c t i", i=TOKEN_RUN),
             )
+            if with_negative:
+                negated = stage.tile([P, HALF * PACK], BF16, name="negated", align_bytes=64)
+                nc.vector.tensor_scalar(
+                    out=negated[:],
+                    in0=packed[:, 0 : HALF * PACK],
+                    scalar1=-1.0,
+                    scalar2=None,
+                    op0=ALU.mult,
+                )
+            sample["mx"] = quantise(packed[:], ROWS, sample["name"])
+            if with_negative:
+                sample["negative_mx"] = quantise(negated[:], HALF, "neg" + sample["name"])
 
-        def projection_steps(sample):
-            passes = [lambda t=t: project_plane(sample, t, False) for t in range(PACK)]
-            return passes + [lambda: pack_features(sample, False)]
-
-        steps = projection_steps(q[1]) + projection_steps(k[1])
-        for s in range(2, SAMPLES):
-            for sample in (q[s], k[s]):
-                steps.extend(rows_steps(sample) + projection_steps(sample))
-
-        pair_order = []
+        matrices = [wq, wk]
         for s in range(SAMPLES):
-            pair_order.extend((a, s) for a in range(s + 1))
-            if s + 1 < SAMPLES:
-                pair_order.extend((s + 1, b) for b in range(s + 1))
+            matrices.extend((q[s], k[s]))
+        weights = 2
+        for i in range(len(matrices) + 2):
+            if i < len(matrices):
+                flip_rows(matrices[i])
+            if i - 2 >= weights:
+                quantise_features(matrices[i - 2], (i - 2) % 2 == 0)
+            if i < len(matrices):
+                quantise_rows(matrices[i])
+            if weights <= i - 1 < len(matrices):
+                project(matrices[i - 1], (i - 1) % 2 == 0)
 
         waiting = []
+        folded = []
 
         def take_maximum():
             logits, column = waiting.pop(0)
@@ -195,36 +181,60 @@ def tile_attention_pa_kernel(
                 out=maxima[:, column : column + 1], in_=logits[:], axis=AXIS.X, op=ALU.max
             )
 
-        for a, b in pair_order:
-            for sample in (q[a], k[b]):
-                if "mx" not in sample:
-                    while sample in (q[1], k[1]) and len(waiting) > 1:
-                        take_maximum()
-                    quantise_features(sample)
-            for side, (stationary, moving) in enumerate(((q[a], k[b]), (k[b], q[a]))):
-                s_codes, s_scales = stationary["mx"]
-                m_codes, m_scales = moving["mx"]
-                for block in range(BLOCKS):
-                    cols = slice(block * P, (block + 1) * P)
-                    logits = banks.tile([P, ROWS], F32, name="logits", tag="bank")
+        def take_folded_maxima():
+            larger, column = folded.pop(0)
+            nc.vector.tensor_reduce(
+                out=maxima[:, column : column + BLOCKS], in_=larger[:], axis=AXIS.X, op=ALU.max
+            )
+
+        for pair in range(PAIRS):
+            q_codes, q_scales = q[pair // SAMPLES]["mx"]
+            n_codes, n_scales = q[pair // SAMPLES]["negative_mx"]
+            k_codes, k_scales = k[pair % SAMPLES]["mx"]
+            first = slice(0, HALF)
+            last = slice(HALF, ROWS)
+            lower = folds.tile([P, BLOCKS, HALF], F32, name="lower")
+            larger = folds.tile([P, BLOCKS, HALF], F32, name="larger")
+            for block in range(BLOCKS):
+                cols = slice(block * P, (block + 1) * P)
+                logits = banks.tile([P, ROWS], F32, name="logits", tag="bank")
+                nc.tensor.matmul_mx(
+                    out=logits[:],
+                    lhsT=q_codes[:, cols].bitcast(FP8X4),
+                    lhsT_scale=q_scales[:, cols],
+                    rhs=k_codes[:].bitcast(FP8X4),
+                    rhs_scale=k_scales[:],
+                    start=True,
+                    stop=True,
+                )
+                waiting.append((logits, pair * MAXIMA + block))
+                halves = banks.tile([P, 2, HALF], F32, name="halves", tag="bank")
+                for target, codes, scales, tokens, start, stop in (
+                    (0, q_codes, q_scales, first, True, True),
+                    (1, q_codes, q_scales, last, True, False),
+                    (1, n_codes, n_scales, first, False, True),
+                ):
                     nc.tensor.matmul_mx(
-                        out=logits[:],
-                        lhsT=s_codes[:, cols].bitcast(FP8X4),
-                        lhsT_scale=s_scales[:, cols],
-                        rhs=m_codes[:].bitcast(FP8X4),
-                        rhs_scale=m_scales[:],
-                        start=True,
-                        stop=True,
+                        out=halves[:, target, :],
+                        lhsT=k_codes[:, cols].bitcast(FP8X4),
+                        lhsT_scale=k_scales[:, cols],
+                        rhs=codes[:, tokens].bitcast(FP8X4),
+                        rhs_scale=scales[:, tokens],
+                        start=start,
+                        stop=stop,
                     )
-                    waiting.append((logits, (a * SAMPLES + b) * MAXIMA + side * BLOCKS + block))
-                    if steps:
-                        step = steps.pop(0)
-                        if step is not None:
-                            step()
-                    if len(waiting) > LOOKAHEAD:
-                        take_maximum()
+                nc.scalar.copy(out=lower[:, block, :], in_=halves[:, 0, :])
+                nc.scalar.activation(out=larger[:, block, :], in_=halves[:, 1, :], func=ACT.Relu)
+                if len(waiting) > LOOKAHEAD:
+                    take_maximum()
+            nc.gpsimd.tensor_tensor(out=larger[:], in0=larger[:], in1=lower[:], op=ALU.add)
+            folded.append((larger, pair * MAXIMA + BLOCKS))
+            if len(folded) > FOLD_LAG:
+                take_folded_maxima()
         while waiting:
             take_maximum()
+        while folded:
+            take_folded_maxima()
 
         sums = keep.tile([P, PAIRS], F32, name="sums")
         nc.vector.tensor_reduce(

@@ -139,12 +139,13 @@ def tile_attention_pa_kernel(
                         out=plane, in_=acc[:], func=ACT.Identity, bias=bias, scale=1.0
                     )
 
-        def quantise_features(sample, with_negative):
+        def pack_features(sample, with_negative):
             packed = stage.tile([P, ROWS * PACK], BF16, name="packed", align_bytes=64)
             nc.vector.tensor_copy(
                 out=packed[:].rearrange("p (c i t) -> p c t i", i=TOKEN_RUN, t=PACK),
                 in_=sample["planes"][:].rearrange("p t (c i) -> p c t i", i=TOKEN_RUN),
             )
+            sample["packed"] = packed
             if with_negative:
                 negated = stage.tile([P, HALF * PACK], BF16, name="negated", align_bytes=64)
                 nc.vector.tensor_scalar(
@@ -154,19 +155,26 @@ def tile_attention_pa_kernel(
                     scalar2=None,
                     op0=ALU.mult,
                 )
-            sample["mx"] = quantise(packed[:], ROWS, sample["name"])
+                sample["negated"] = negated
+
+        def quantise_features(sample, with_negative):
+            sample["mx"] = quantise(sample["packed"][:], ROWS, sample["name"])
             if with_negative:
-                sample["negative_mx"] = quantise(negated[:], HALF, "neg" + sample["name"])
+                sample["negative_mx"] = quantise(
+                    sample["negated"][:], HALF, "neg" + sample["name"]
+                )
 
         matrices = [wq, wk]
         for s in range(SAMPLES):
             matrices.extend((q[s], k[s]))
         weights = 2
-        for i in range(len(matrices) + 2):
+        for i in range(len(matrices) + 3):
             if i < len(matrices):
                 flip_rows(matrices[i])
-            if i - 2 >= weights:
-                quantise_features(matrices[i - 2], (i - 2) % 2 == 0)
+            if weights <= i - 2 < len(matrices):
+                pack_features(matrices[i - 2], (i - 2) % 2 == 0)
+            if weights <= i - 3:
+                quantise_features(matrices[i - 3], (i - 3) % 2 == 0)
             if i < len(matrices):
                 quantise_rows(matrices[i])
             if weights <= i - 1 < len(matrices):

@@ -27,7 +27,21 @@ STORE_RUN = 8
 TOKEN_RUN = 4
 
 PSUM_BANKS = 8
-LOOKAHEAD = PSUM_BANKS // 2
+LOOKAHEAD = 4
+PIECES = (1, 1)
+LAG = 2
+SHARED_FLIPS = 0
+FIRST_ROUND = 13
+ST = (2, 2, 2)
+FUSED = ()
+LASTV = ('q0', 'q1', 'q2', 'q3')
+NEG = {"q0": True, "q1": True, "q2": True, "q3": True, "k0": False, "k1": False, "k2": False, "k3": False}
+FOLDS = ((4, 1), (4, 1), (4, 1), (4, 1))
+LAST_FOLDS = ((4, 1),)
+
+
+MOST_FOLDS = 6
+
 FOLD_LAG = 2
 
 FLOPS = 2 * (2 * SAMPLES * ROWS) * FEATURES * FEATURES + 2 * (SAMPLES * ROWS) ** 2 * FEATURES
@@ -52,15 +66,21 @@ def tile_attention_pa_kernel(
             nc.scalar.dma_start(out=narrow[:], in_=vector.rearrange("(p t) -> p t", t=PACK))
             return narrow
 
-        def load_matrix(matrix, name):
+        def load_matrix(matrix, name, pieces=1):
             raw = keep.tile([P, BLOCKS * FEATURES], BF16, name=name + "_raw")
-            nc.sync.dma_start(out=raw[:], in_=matrix.rearrange("(p r) f -> p (r f)", r=BLOCKS))
+            rows = matrix.rearrange("(p r) f -> p r f", r=BLOCKS)
+            by_row = raw[:].rearrange("p (r f) -> p r f", r=BLOCKS)
+            count = BLOCKS // pieces
+            for first in range(0, BLOCKS, count):
+                nc.sync.dma_start(
+                    out=by_row[:, first : first + count, :], in_=rows[:, first : first + count, :]
+                )
             return {"name": name, "raw": raw}
 
         bq_bf16 = load_bias(bq, "bq_bf16")
         bk_bf16 = load_bias(bk, "bk_bf16")
-        wq = load_matrix(Wq, "wq")
-        wk = load_matrix(Wk, "wk")
+        wq = load_matrix(Wq, "wq", PIECES[0])
+        wk = load_matrix(Wk, "wk", PIECES[1])
         q = []
         k = []
         for s in range(SAMPLES):
@@ -90,62 +110,96 @@ def tile_attention_pa_kernel(
             nc.vector.quantize_mx(out=codes[:].bitcast(FP8X4), scales=scales[:], in_=values)
             return codes, scales
 
-        def flip_rows(mat):
-            mat["grouped"] = stage.tile([P, ROWS * PACK], BF16, name="grouped", align_bytes=64)
+        def flip_half(mat, half, on_vector):
+            if half == 0:
+                mat["grouped"] = stage.tile(
+                    [P, ROWS * PACK], BF16, name="grouped", align_bytes=64
+                )
             words = mat["raw"][:].bitcast(F32)
             grouped_words = mat["grouped"][:].bitcast(F32).rearrange("p (c u) -> p c u", u=PLANES)
-            for half in range(ROWS // HALF):
-                flipped = banks.tile([P, PLANES, HALF], F32, name="flipped", tag="bank")
-                for r in range(HALF // P):
-                    first_word = (half * (HALF // P) + r) * WORDS
-                    for u in range(PLANES):
-                        nc.tensor.transpose(
-                            flipped[:, u, r * P : (r + 1) * P],
-                            words[:, first_word + u * P : first_word + (u + 1) * P],
-                            identity[:],
-                        )
-                nc.scalar.copy(
-                    out=grouped_words[:, half * HALF : (half + 1) * HALF, :],
-                    in_=flipped[:].rearrange("p u c -> p c u"),
-                )
+            flipped = banks.tile([P, PLANES, HALF], F32, name="flipped", tag="bank")
+            for r in range(HALF // P):
+                first_word = (half * (HALF // P) + r) * WORDS
+                for u in range(PLANES):
+                    nc.tensor.transpose(
+                        flipped[:, u, r * P : (r + 1) * P],
+                        words[:, first_word + u * P : first_word + (u + 1) * P],
+                        identity[:],
+                    )
+            copy = nc.vector.tensor_copy if on_vector else nc.scalar.copy
+            copy(
+                out=grouped_words[:, half * HALF : (half + 1) * HALF, :],
+                in_=flipped[:].rearrange("p u c -> p c u"),
+            )
 
         def quantise_rows(mat):
             mat["rows_mx"] = quantise(mat["grouped"][:], ROWS, "x" + mat["name"])
 
-        def project(sample, last_on_vector):
-            sample["planes"] = stage.tile([P, PACK, ROWS], BF16, name="planes")
+        def project_plane(sample, t):
+            if t == 0:
+                sample["planes"] = stage.tile([P, PACK, ROWS], BF16, name="planes")
             w_codes, w_scales = sample["weight"]["rows_mx"]
             x_codes, x_scales = sample["rows_mx"]
+            cols = slice(t * P, (t + 1) * P)
+            acc = banks.tile([P, ROWS], F32, name="acc", tag="bank")
+            nc.tensor.matmul_mx(
+                out=acc[:],
+                lhsT=w_codes[:, cols].bitcast(FP8X4),
+                lhsT_scale=w_scales[:, cols],
+                rhs=x_codes[:].bitcast(FP8X4),
+                rhs_scale=x_scales[:],
+                start=True,
+                stop=True,
+            )
+            plane = sample["planes"][:, t, :]
+            bias = sample["bias"][:, t : t + 1]
+            if sample["name"] in LASTV and t == PACK - 1:
+                nc.vector.tensor_scalar(
+                    out=plane, in0=acc[:], scalar1=bias, scalar2=None, op0=ALU.add
+                )
+            else:
+                nc.scalar.activation(
+                    out=plane, in_=acc[:], func=ACT.Identity, bias=bias, scale=1.0
+                )
+
+        def project_chunk(sample, chunk):
+            if chunk == 0:
+                sample["packed"] = stage.tile(
+                    [P, ROWS * PACK], BF16, name="packed", align_bytes=64
+                )
+            w_codes, w_scales = sample["weight"]["rows_mx"]
+            x_codes, x_scales = sample["rows_mx"]
+            tokens = slice(chunk * P, (chunk + 1) * P)
+            acc = banks.tile([P, PACK, P], F32, name="acc", tag="bank")
             for t in range(PACK):
                 cols = slice(t * P, (t + 1) * P)
-                acc = banks.tile([P, ROWS], F32, name="acc", tag="bank")
                 nc.tensor.matmul_mx(
-                    out=acc[:],
+                    out=acc[:, t, :],
                     lhsT=w_codes[:, cols].bitcast(FP8X4),
                     lhsT_scale=w_scales[:, cols],
-                    rhs=x_codes[:].bitcast(FP8X4),
-                    rhs_scale=x_scales[:],
+                    rhs=x_codes[:, tokens].bitcast(FP8X4),
+                    rhs_scale=x_scales[:, tokens],
                     start=True,
                     stop=True,
                 )
-                plane = sample["planes"][:, t, :]
-                bias = sample["bias"][:, t : t + 1]
-                if last_on_vector and t == PACK - 1:
-                    nc.vector.tensor_scalar(
-                        out=plane, in0=acc[:], scalar1=bias, scalar2=None, op0=ALU.add
-                    )
-                else:
-                    nc.scalar.activation(
-                        out=plane, in_=acc[:], func=ACT.Identity, bias=bias, scale=1.0
-                    )
+            words = sample["packed"][:, chunk * P * PACK : (chunk + 1) * P * PACK]
+            nc.vector.tensor_tensor(
+                out=words.rearrange("p (c t) -> p c t", t=PACK),
+                in0=acc[:].rearrange("p t c -> p c t"),
+                in1=sample["bias"][:].unsqueeze(1).to_broadcast([P, P, PACK]),
+                op=ALU.add,
+            )
 
         def pack_features(sample, with_negative):
-            packed = stage.tile([P, ROWS * PACK], BF16, name="packed", align_bytes=64)
-            nc.vector.tensor_copy(
-                out=packed[:].rearrange("p (c i t) -> p c t i", i=TOKEN_RUN, t=PACK),
-                in_=sample["planes"][:].rearrange("p t (c i) -> p c t i", i=TOKEN_RUN),
-            )
-            sample["packed"] = packed
+            if sample["name"] in FUSED:
+                packed = sample["packed"]
+            else:
+                packed = stage.tile([P, ROWS * PACK], BF16, name="packed", align_bytes=64)
+                nc.vector.tensor_copy(
+                    out=packed[:].rearrange("p (c i t) -> p c t i", i=TOKEN_RUN, t=PACK),
+                    in_=sample["planes"][:].rearrange("p t (c i) -> p c t i", i=TOKEN_RUN),
+                )
+                sample["packed"] = packed
             if with_negative:
                 negated = stage.tile([P, HALF * PACK], BF16, name="negated", align_bytes=64)
                 nc.vector.tensor_scalar(
@@ -168,17 +222,36 @@ def tile_attention_pa_kernel(
         for s in range(SAMPLES):
             matrices.extend((q[s], k[s]))
         weights = 2
-        for i in range(len(matrices) + 3):
+
+        def stage_round(i):
+            steps = [[] for step in range(MAXIMA)]
             if i < len(matrices):
-                flip_rows(matrices[i])
-            if weights <= i - 2 < len(matrices):
-                pack_features(matrices[i - 2], (i - 2) % 2 == 0)
-            if weights <= i - 3:
-                quantise_features(matrices[i - 3], (i - 3) % 2 == 0)
+                shared = i < SHARED_FLIPS
+                for half in range(2):
+                    steps[half + 0].append((flip_half, matrices[i], half, shared and half == 1))
+            lag = LAG
+            if weights <= i - lag < len(matrices):
+                steps[ST[0]].append((pack_features, matrices[i - lag], NEG[matrices[i - lag]["name"]]))
+            if weights <= i - lag - 1 < len(matrices):
+                steps[ST[1]].append((quantise_features, matrices[i - lag - 1], NEG[matrices[i - lag - 1]["name"]]))
             if i < len(matrices):
-                quantise_rows(matrices[i])
+                steps[ST[2]].append((quantise_rows, matrices[i]))
             if weights <= i - 1 < len(matrices):
-                project(matrices[i - 1], (i - 1) % 2 == 0)
+                sample = matrices[i - 1]
+                for t in range(PACK):
+                    if sample["name"] in FUSED:
+                        steps[3 + t].append((project_chunk, sample, t))
+                    else:
+                        steps[3 + t].append((project_plane, sample, t))
+            return steps
+
+        for i in range(FIRST_ROUND):
+            for calls in stage_round(i):
+                for call in calls:
+                    call[0](*call[1:])
+        chores = []
+        for i in range(FIRST_ROUND, len(matrices) + LAG + 1):
+            chores.extend(stage_round(i))
 
         waiting = []
         folded = []
@@ -190,57 +263,101 @@ def tile_attention_pa_kernel(
             )
 
         def take_folded_maxima():
-            larger, column = folded.pop(0)
+            larger, column, count = folded.pop(0)
             nc.vector.tensor_reduce(
-                out=maxima[:, column : column + BLOCKS], in_=larger[:], axis=AXIS.X, op=ALU.max
+                out=maxima[:, column : column + count],
+                in_=larger[:, 0:count, :],
+                axis=AXIS.X,
+                op=ALU.max,
             )
 
-        for pair in range(PAIRS):
-            q_codes, q_scales = q[pair // SAMPLES]["mx"]
-            n_codes, n_scales = q[pair // SAMPLES]["negative_mx"]
-            k_codes, k_scales = k[pair % SAMPLES]["mx"]
+        def plain_logits(rows, columns, block, column):
+            cols = slice(block * P, (block + 1) * P)
+            codes, scales = rows["mx"]
+            all_codes, all_scales = columns["mx"]
+            logits = banks.tile([P, ROWS], F32, name="logits", tag="bank")
+            nc.tensor.matmul_mx(
+                out=logits[:],
+                lhsT=codes[:, cols].bitcast(FP8X4),
+                lhsT_scale=scales[:, cols],
+                rhs=all_codes[:].bitcast(FP8X4),
+                rhs_scale=all_scales[:],
+                start=True,
+                stop=True,
+            )
+            waiting.append((logits, column))
+
+        def folded_logits(rows, columns, block, column, fold):
+            cols = slice(block * P, (block + 1) * P)
+            codes, scales = rows["mx"]
+            all_codes, all_scales = columns["mx"]
+            if "negative_mx" in columns:
+                negative = (codes, scales) + columns["negative_mx"]
+            else:
+                negative = rows["negative_mx"] + (all_codes, all_scales)
             first = slice(0, HALF)
             last = slice(HALF, ROWS)
-            lower = folds.tile([P, BLOCKS, HALF], F32, name="lower")
-            larger = folds.tile([P, BLOCKS, HALF], F32, name="larger")
-            for block in range(BLOCKS):
-                cols = slice(block * P, (block + 1) * P)
-                logits = banks.tile([P, ROWS], F32, name="logits", tag="bank")
+            halves = banks.tile([P, 2, HALF], F32, name="halves", tag="bank")
+            positive = (codes, scales, all_codes, all_scales)
+            for target, operands, tokens, start, stop in (
+                (0, positive, first, True, True),
+                (1, positive, last, True, False),
+                (1, negative, first, False, True),
+            ):
+                still, still_scales, moving, moving_scales = operands
                 nc.tensor.matmul_mx(
-                    out=logits[:],
-                    lhsT=q_codes[:, cols].bitcast(FP8X4),
-                    lhsT_scale=q_scales[:, cols],
-                    rhs=k_codes[:].bitcast(FP8X4),
-                    rhs_scale=k_scales[:],
-                    start=True,
-                    stop=True,
+                    out=halves[:, target, :],
+                    lhsT=still[:, cols].bitcast(FP8X4),
+                    lhsT_scale=still_scales[:, cols],
+                    rhs=moving[:, tokens].bitcast(FP8X4),
+                    rhs_scale=moving_scales[:, tokens],
+                    start=start,
+                    stop=stop,
                 )
-                waiting.append((logits, pair * MAXIMA + block))
-                halves = banks.tile([P, 2, HALF], F32, name="halves", tag="bank")
-                for target, codes, scales, tokens, start, stop in (
-                    (0, q_codes, q_scales, first, True, True),
-                    (1, q_codes, q_scales, last, True, False),
-                    (1, n_codes, n_scales, first, False, True),
-                ):
-                    nc.tensor.matmul_mx(
-                        out=halves[:, target, :],
-                        lhsT=k_codes[:, cols].bitcast(FP8X4),
-                        lhsT_scale=k_scales[:, cols],
-                        rhs=codes[:, tokens].bitcast(FP8X4),
-                        rhs_scale=scales[:, tokens],
-                        start=start,
-                        stop=stop,
-                    )
-                nc.scalar.copy(out=lower[:, block, :], in_=halves[:, 0, :])
-                nc.scalar.activation(out=larger[:, block, :], in_=halves[:, 1, :], func=ACT.Relu)
+            lower, larger, side, count = fold
+            nc.scalar.copy(out=lower[:, side, :], in_=halves[:, 0, :])
+            nc.scalar.activation(out=larger[:, side, :], in_=halves[:, 1, :], func=ACT.Relu)
+            if side == count - 1:
+                nc.gpsimd.tensor_tensor(
+                    out=larger[:, 0:count, :],
+                    in0=larger[:, 0:count, :],
+                    in1=lower[:, 0:count, :],
+                    op=ALU.add,
+                )
+                folded.append((larger, column - side, count))
+                if len(folded) > FOLD_LAG:
+                    take_folded_maxima()
+
+        pairs = [(a, b) for a in range(SAMPLES) for b in range(SAMPLES)]
+        for n, (a, b) in enumerate(pairs):
+            by_key, by_query = FOLDS[b]
+            if n >= PAIRS - len(LAST_FOLDS):
+                by_key, by_query = LAST_FOLDS[n - PAIRS]
+            base = (a * SAMPLES + b) * MAXIMA
+            folds_here = [(q[a], k[b], i, base + BLOCKS - 1 - i) for i in reversed(range(by_query))]
+            folds_here += [(k[b], q[a], i, base + BLOCKS + i) for i in range(by_key)]
+            plain = [(q[a], k[b], i, base + BLOCKS - 1 - i) for i in range(by_query, BLOCKS)]
+            plain += [(k[b], q[a], i, base + BLOCKS + i) for i in range(by_key, BLOCKS)]
+            fold_count = len(folds_here)
+            if fold_count:
+                lower = folds.tile([P, MOST_FOLDS, HALF], F32, name="lower")
+                larger = folds.tile([P, MOST_FOLDS, HALF], F32, name="larger")
+            plain_count = len(plain)
+            for i in range(MAXIMA):
+                if chores:
+                    for call in chores.pop(0):
+                        call[0](*call[1:])
+                if (i >= MAXIMA - plain_count if n == PAIRS - 1 else -(-(i + 1) * plain_count // MAXIMA) > -(-i * plain_count // MAXIMA)):
+                    plain_logits(*plain.pop(0))
+                else:
+                    side = fold_count - len(folds_here)
+                    folded_logits(*folds_here.pop(0), (lower, larger, side, fold_count))
                 if len(waiting) > LOOKAHEAD:
                     take_maximum()
-            nc.gpsimd.tensor_tensor(out=larger[:], in0=larger[:], in1=lower[:], op=ALU.add)
-            folded.append((larger, pair * MAXIMA + BLOCKS))
-            if len(folded) > FOLD_LAG:
-                take_folded_maxima()
         while waiting:
             take_maximum()
+            if folded:
+                take_folded_maxima()
         while folded:
             take_folded_maxima()
 

@@ -32,17 +32,17 @@ PIECES = (1, 1)
 LAG = 2
 SHARED_FLIPS = 0
 FIRST_ROUND = 13
-ST = (2, 2, 2)
+ST = (2, 2, 3, 3)
 FUSED = ()
 LASTV = ('q0', 'q1', 'q2', 'q3')
 NEG = {"q0": True, "q1": True, "q2": True, "q3": True, "k0": False, "k1": False, "k2": False, "k3": False}
 FOLDS = ((4, 1), (4, 1), (4, 1), (4, 1))
-LAST_FOLDS = ((4, 1),)
+LAST_FOLDS = ((2, 0),)
 
 
 MOST_FOLDS = 6
 
-FOLD_LAG = 2
+FOLD_LAG = 3
 
 FLOPS = 2 * (2 * SAMPLES * ROWS) * FEATURES * FEATURES + 2 * (SAMPLES * ROWS) ** 2 * FEATURES
 
@@ -190,26 +190,26 @@ def tile_attention_pa_kernel(
                 op=ALU.add,
             )
 
-        def pack_features(sample, with_negative):
+        def pack_features(sample):
             if sample["name"] in FUSED:
-                packed = sample["packed"]
-            else:
-                packed = stage.tile([P, ROWS * PACK], BF16, name="packed", align_bytes=64)
-                nc.vector.tensor_copy(
-                    out=packed[:].rearrange("p (c i t) -> p c t i", i=TOKEN_RUN, t=PACK),
-                    in_=sample["planes"][:].rearrange("p t (c i) -> p c t i", i=TOKEN_RUN),
-                )
-                sample["packed"] = packed
-            if with_negative:
-                negated = stage.tile([P, HALF * PACK], BF16, name="negated", align_bytes=64)
-                nc.vector.tensor_scalar(
-                    out=negated[:],
-                    in0=packed[:, 0 : HALF * PACK],
-                    scalar1=-1.0,
-                    scalar2=None,
-                    op0=ALU.mult,
-                )
-                sample["negated"] = negated
+                return
+            packed = stage.tile([P, ROWS * PACK], BF16, name="packed", align_bytes=64)
+            nc.vector.tensor_copy(
+                out=packed[:].rearrange("p (c i t) -> p c t i", i=TOKEN_RUN, t=PACK),
+                in_=sample["planes"][:].rearrange("p t (c i) -> p c t i", i=TOKEN_RUN),
+            )
+            sample["packed"] = packed
+
+        def negate_features(sample):
+            negated = stage.tile([P, HALF * PACK], BF16, name="negated", align_bytes=64)
+            nc.vector.tensor_scalar(
+                out=negated[:],
+                in0=sample["packed"][:, 0 : HALF * PACK],
+                scalar1=-1.0,
+                scalar2=None,
+                op0=ALU.mult,
+            )
+            sample["negated"] = negated
 
         def quantise_features(sample, with_negative):
             sample["mx"] = quantise(sample["packed"][:], ROWS, sample["name"])
@@ -231,7 +231,9 @@ def tile_attention_pa_kernel(
                     steps[half + 0].append((flip_half, matrices[i], half, shared and half == 1))
             lag = LAG
             if weights <= i - lag < len(matrices):
-                steps[ST[0]].append((pack_features, matrices[i - lag], NEG[matrices[i - lag]["name"]]))
+                steps[ST[0]].append((pack_features, matrices[i - lag]))
+                if NEG[matrices[i - lag]["name"]]:
+                    steps[ST[3]].append((negate_features, matrices[i - lag]))
             if weights <= i - lag - 1 < len(matrices):
                 steps[ST[1]].append((quantise_features, matrices[i - lag - 1], NEG[matrices[i - lag - 1]["name"]]))
             if i < len(matrices):

@@ -28,16 +28,16 @@ TOKEN_RUN = 4
 
 PSUM_BANKS = 8
 LOOKAHEAD = 4
-PIECES = (1, 1)
+PIECES = (2, 2)
 LAG = 2
-SHARED_FLIPS = 0
+SHARED_FLIPS = 1
 FIRST_ROUND = 13
 ST = (2, 2, 3, 3)
-FUSED = ()
-LASTV = ('q0', 'q1', 'q2', 'q3')
+FUSED = ('q0', 'k0')
+LASTV = ('q2', 'q3')
 NEG = {"q0": True, "q1": True, "q2": True, "q3": True, "k0": False, "k1": False, "k2": False, "k3": False}
 FOLDS = ((4, 1), (4, 1), (4, 1), (4, 1))
-LAST_FOLDS = ((2, 0),)
+LAST_FOLDS = ((4, 0),)
 
 
 MOST_FOLDS = 6
@@ -349,7 +349,7 @@ def tile_attention_pa_kernel(
                 if chores:
                     for call in chores.pop(0):
                         call[0](*call[1:])
-                if (i >= MAXIMA - plain_count if n == PAIRS - 1 else -(-(i + 1) * plain_count // MAXIMA) > -(-i * plain_count // MAXIMA)):
+                if (i % 2 == 1 or not folds_here if n == PAIRS - 1 else -(-(i + 1) * plain_count // MAXIMA) > -(-i * plain_count // MAXIMA)):
                     plain_logits(*plain.pop(0))
                 else:
                     side = fold_count - len(folds_here)

@@ -32,7 +32,7 @@ PIECES = (2, 2)
 LAG = 2
 SHARED_FLIPS = 1
 FIRST_ROUND = 13
-ST = (2, 2, 3, 3)
+ST = (1, 0, 2, 3)
 FUSED = ('q0', 'k0')
 LASTV = ('q2', 'q3')
 NEG = {"q0": True, "q1": True, "q2": True, "q3": True, "k0": False, "k1": False, "k2": False, "k3": False}

from contextlib import ExitStack

import concourse.mybir as mybir
from concourse.masks import make_identity

F32 = mybir.dt.float32
BF16 = mybir.dt.bfloat16
U32 = mybir.dt.uint32
U8 = mybir.dt.uint8
FP8X4 = mybir.dt.float8_e4m3fn_x4
ACT = mybir.ActivationFunctionType
ALU = mybir.AluOpType
AXIS = mybir.AxisListType

P = 128
PACK = 4
SAMPLES = 4
ROWS = 512
FEATURES = 512
BLOCKS = ROWS // P
WORDS = FEATURES // 2
PLANES = WORDS // P
HALF = ROWS // 2
PAIRS = SAMPLES * SAMPLES
MAXIMA = 2 * BLOCKS
STORE_RUN = 8
TOKEN_RUN = 4

PSUM_BANKS = 8
LOOKAHEAD = 4
PIECES = (2, 2)
LAG = 2
SHARED_FLIPS = 1
FIRST_ROUND = 13
ST = (1, 0, 2, 3)
FUSED = ('q0', 'k0')
LASTV = ('q2', 'q3')
NEG = {"q0": True, "q1": True, "q2": True, "q3": True, "k0": False, "k1": False, "k2": False, "k3": False}
FOLDS = ((4, 1), (4, 1), (4, 1), (4, 1))
LAST_FOLDS = ((4, 0),)


MOST_FOLDS = 6

FOLD_LAG = 3

FLOPS = 2 * (2 * SAMPLES * ROWS) * FEATURES * FEATURES + 2 * (SAMPLES * ROWS) ** 2 * FEATURES


def tile_attention_pa_kernel(
    tc, query_states, key_states, Wq, bq, Wk, bk, logit_scale, out
):
    nc = tc.nc
    with ExitStack() as ctx:
        ctx.enter_context(tc.manual_schedule())
        keep = ctx.enter_context(tc.tile_pool(name="keep", bufs=1))
        stage = ctx.enter_context(tc.tile_pool(name="stage", bufs=3))
        folds = ctx.enter_context(tc.tile_pool(name="folds", bufs=FOLD_LAG + 2))
        banks = ctx.enter_context(tc.psum_pool(name="banks", bufs=PSUM_BANKS))

        log_gain = keep.tile([P, 1], BF16, name="log_gain")
        nc.scalar.dma_start(out=log_gain[:], in_=logit_scale.partition_broadcast(P))

        def load_bias(vector, name):
            narrow = keep.tile([P, PACK], BF16, name=name)
            nc.scalar.dma_start(out=narrow[:], in_=vector.rearrange("(p t) -> p t", t=PACK))
            return narrow

        def load_matrix(matrix, name, pieces=1):
            raw = keep.tile([P, BLOCKS * FEATURES], BF16, name=name + "_raw")
            rows = matrix.rearrange("(p r) f -> p r f", r=BLOCKS)
            by_row = raw[:].rearrange("p (r f) -> p r f", r=BLOCKS)
            count = BLOCKS // pieces
            for first in range(0, BLOCKS, count):
                nc.sync.dma_start(
                    out=by_row[:, first : first + count, :], in_=rows[:, first : first + count, :]
                )
            return {"name": name, "raw": raw}

        bq_bf16 = load_bias(bq, "bq_bf16")
        bk_bf16 = load_bias(bk, "bk_bf16")
        wq = load_matrix(Wq, "wq", PIECES[0])
        wk = load_matrix(Wk, "wk", PIECES[1])
        q = []
        k = []
        for s in range(SAMPLES):
            q.append(load_matrix(query_states[s], "q%d" % s))
            k.append(load_matrix(key_states[s], "k%d" % s))

        identity = keep.tile([P, P], F32, name="identity")
        make_identity(nc, identity[:])
        ones = keep.tile([P, P], F32, name="ones")
        nc.vector.memset(ones[:], 1.0)
        gain = keep.tile([P, 1], F32, name="gain")
        nc.scalar.activation(out=gain[:], in_=log_gain[:], func=ACT.Exp)
        bq_f32 = keep.tile([P, PACK], F32, name="bq_f32")
        nc.vector.tensor_copy(out=bq_f32[:], in_=bq_bf16[:])
        bk_f32 = keep.tile([P, PACK], F32, name="bk_f32")
        nc.vector.tensor_copy(out=bk_f32[:], in_=bk_bf16[:])
        for s in range(SAMPLES):
            q[s]["weight"] = wq
            q[s]["bias"] = bq_f32
            k[s]["weight"] = wk
            k[s]["bias"] = bk_f32
        maxima = keep.tile([P, PAIRS * MAXIMA], F32, name="maxima")

        def quantise(values, columns, name):
            codes = keep.tile([P, columns], U32, name=name + "_codes", align_bytes=64)
            scales = keep.tile([P, columns], U8, name=name + "_scales", align_bytes=64)
            nc.vector.quantize_mx(out=codes[:].bitcast(FP8X4), scales=scales[:], in_=values)
            return codes, scales

        def flip_half(mat, half, on_vector):
            if half == 0:
                mat["grouped"] = stage.tile(
                    [P, ROWS * PACK], BF16, name="grouped", align_bytes=64
                )
            words = mat["raw"][:].bitcast(F32)
            grouped_words = mat["grouped"][:].bitcast(F32).rearrange("p (c u) -> p c u", u=PLANES)
            flipped = banks.tile([P, PLANES, HALF], F32, name="flipped", tag="bank")
            for r in range(HALF // P):
                first_word = (half * (HALF // P) + r) * WORDS
                for u in range(PLANES):
                    nc.tensor.transpose(
                        flipped[:, u, r * P : (r + 1) * P],
                        words[:, first_word + u * P : first_word + (u + 1) * P],
                        identity[:],
                    )
            copy = nc.vector.tensor_copy if on_vector else nc.scalar.copy
            copy(
                out=grouped_words[:, half * HALF : (half + 1) * HALF, :],
                in_=flipped[:].rearrange("p u c -> p c u"),
            )

        def quantise_rows(mat):
            mat["rows_mx"] = quantise(mat["grouped"][:], ROWS, "x" + mat["name"])

        def project_plane(sample, t):
            if t == 0:
                sample["planes"] = stage.tile([P, PACK, ROWS], BF16, name="planes")
            w_codes, w_scales = sample["weight"]["rows_mx"]
            x_codes, x_scales = sample["rows_mx"]
            cols = slice(t * P, (t + 1) * P)
            acc = banks.tile([P, ROWS], F32, name="acc", tag="bank")
            nc.tensor.matmul_mx(
                out=acc[:],
                lhsT=w_codes[:, cols].bitcast(FP8X4),
                lhsT_scale=w_scales[:, cols],
                rhs=x_codes[:].bitcast(FP8X4),
                rhs_scale=x_scales[:],
                start=True,
                stop=True,
            )
            plane = sample["planes"][:, t, :]
            bias = sample["bias"][:, t : t + 1]
            if sample["name"] in LASTV and t == PACK - 1:
                nc.vector.tensor_scalar(
                    out=plane, in0=acc[:], scalar1=bias, scalar2=None, op0=ALU.add
                )
            else:
                nc.scalar.activation(
                    out=plane, in_=acc[:], func=ACT.Identity, bias=bias, scale=1.0
                )

        def project_chunk(sample, chunk):
            if chunk == 0:
                sample["packed"] = stage.tile(
                    [P, ROWS * PACK], BF16, name="packed", align_bytes=64
                )
            w_codes, w_scales = sample["weight"]["rows_mx"]
            x_codes, x_scales = sample["rows_mx"]
            tokens = slice(chunk * P, (chunk + 1) * P)
            acc = banks.tile([P, PACK, P], F32, name="acc", tag="bank")
            for t in range(PACK):
                cols = slice(t * P, (t + 1) * P)
                nc.tensor.matmul_mx(
                    out=acc[:, t, :],
                    lhsT=w_codes[:, cols].bitcast(FP8X4),
                    lhsT_scale=w_scales[:, cols],
                    rhs=x_codes[:, tokens].bitcast(FP8X4),
                    rhs_scale=x_scales[:, tokens],
                    start=True,
                    stop=True,
                )
            words = sample["packed"][:, chunk * P * PACK : (chunk + 1) * P * PACK]
            nc.vector.tensor_tensor(
                out=words.rearrange("p (c t) -> p c t", t=PACK),
                in0=acc[:].rearrange("p t c -> p c t"),
                in1=sample["bias"][:].unsqueeze(1).to_broadcast([P, P, PACK]),
                op=ALU.add,
            )

        def pack_features(sample):
            if sample["name"] in FUSED:
                return
            packed = stage.tile([P, ROWS * PACK], BF16, name="packed", align_bytes=64)
            nc.vector.tensor_copy(
                out=packed[:].rearrange("p (c i t) -> p c t i", i=TOKEN_RUN, t=PACK),
                in_=sample["planes"][:].rearrange("p t (c i) -> p c t i", i=TOKEN_RUN),
            )
            sample["packed"] = packed

        def negate_features(sample):
            negated = stage.tile([P, HALF * PACK], BF16, name="negated", align_bytes=64)
            nc.vector.tensor_scalar(
                out=negated[:],
                in0=sample["packed"][:, 0 : HALF * PACK],
                scalar1=-1.0,
                scalar2=None,
                op0=ALU.mult,
            )
            sample["negated"] = negated

        def quantise_features(sample, with_negative):
            sample["mx"] = quantise(sample["packed"][:], ROWS, sample["name"])
            if with_negative:
                sample["negative_mx"] = quantise(
                    sample["negated"][:], HALF, "neg" + sample["name"]
                )

        matrices = [wq, wk]
        for s in range(SAMPLES):
            matrices.extend((q[s], k[s]))
        weights = 2

        def stage_round(i):
            steps = [[] for step in range(MAXIMA)]
            if i < len(matrices):
                shared = i < SHARED_FLIPS
                for half in range(2):
                    steps[half + 0].append((flip_half, matrices[i], half, shared and half == 1))
            lag = LAG
            if weights <= i - lag < len(matrices):
                steps[ST[0]].append((pack_features, matrices[i - lag]))
                if NEG[matrices[i - lag]["name"]]:
                    steps[ST[3]].append((negate_features, matrices[i - lag]))
            if weights <= i - lag - 1 < len(matrices):
                steps[ST[1]].append((quantise_features, matrices[i - lag - 1], NEG[matrices[i - lag - 1]["name"]]))
            if i < len(matrices):
                steps[ST[2]].append((quantise_rows, matrices[i]))
            if weights <= i - 1 < len(matrices):
                sample = matrices[i - 1]
                for t in range(PACK):
                    if sample["name"] in FUSED:
                        steps[3 + t].append((project_chunk, sample, t))
                    else:
                        steps[3 + t].append((project_plane, sample, t))
            return steps

        for i in range(FIRST_ROUND):
            for calls in stage_round(i):
                for call in calls:
                    call[0](*call[1:])
        chores = []
        for i in range(FIRST_ROUND, len(matrices) + LAG + 1):
            chores.extend(stage_round(i))

        waiting = []
        folded = []

        def take_maximum():
            logits, column = waiting.pop(0)
            nc.vector.tensor_reduce(
                out=maxima[:, column : column + 1], in_=logits[:], axis=AXIS.X, op=ALU.max
            )

        def take_folded_maxima():
            larger, column, count = folded.pop(0)
            nc.vector.tensor_reduce(
                out=maxima[:, column : column + count],
                in_=larger[:, 0:count, :],
                axis=AXIS.X,
                op=ALU.max,
            )

        def plain_logits(rows, columns, block, column):
            cols = slice(block * P, (block + 1) * P)
            codes, scales = rows["mx"]
            all_codes, all_scales = columns["mx"]
            logits = banks.tile([P, ROWS], F32, name="logits", tag="bank")
            nc.tensor.matmul_mx(
                out=logits[:],
                lhsT=codes[:, cols].bitcast(FP8X4),
                lhsT_scale=scales[:, cols],
                rhs=all_codes[:].bitcast(FP8X4),
                rhs_scale=all_scales[:],
                start=True,
                stop=True,
            )
            waiting.append((logits, column))

        def folded_logits(rows, columns, block, column, fold):
            cols = slice(block * P, (block + 1) * P)
            codes, scales = rows["mx"]
            all_codes, all_scales = columns["mx"]
            if "negative_mx" in columns:
                negative = (codes, scales) + columns["negative_mx"]
            else:
                negative = rows["negative_mx"] + (all_codes, all_scales)
            first = slice(0, HALF)
            last = slice(HALF, ROWS)
            halves = banks.tile([P, 2, HALF], F32, name="halves", tag="bank")
            positive = (codes, scales, all_codes, all_scales)
            for target, operands, tokens, start, stop in (
                (0, positive, first, True, True),
                (1, positive, last, True, False),
                (1, negative, first, False, True),
            ):
                still, still_scales, moving, moving_scales = operands
                nc.tensor.matmul_mx(
                    out=halves[:, target, :],
                    lhsT=still[:, cols].bitcast(FP8X4),
                    lhsT_scale=still_scales[:, cols],
                    rhs=moving[:, tokens].bitcast(FP8X4),
                    rhs_scale=moving_scales[:, tokens],
                    start=start,
                    stop=stop,
                )
            lower, larger, side, count = fold
            nc.scalar.copy(out=lower[:, side, :], in_=halves[:, 0, :])
            nc.scalar.activation(out=larger[:, side, :], in_=halves[:, 1, :], func=ACT.Relu)
            if side == count - 1:
                nc.gpsimd.tensor_tensor(
                    out=larger[:, 0:count, :],
                    in0=larger[:, 0:count, :],
                    in1=lower[:, 0:count, :],
                    op=ALU.add,
                )
                folded.append((larger, column - side, count))
                if len(folded) > FOLD_LAG:
                    take_folded_maxima()

        pairs = [(a, b) for a in range(SAMPLES) for b in range(SAMPLES)]
        for n, (a, b) in enumerate(pairs):
            by_key, by_query = FOLDS[b]
            if n >= PAIRS - len(LAST_FOLDS):
                by_key, by_query = LAST_FOLDS[n - PAIRS]
            base = (a * SAMPLES + b) * MAXIMA
            folds_here = [(q[a], k[b], i, base + BLOCKS - 1 - i) for i in reversed(range(by_query))]
            folds_here += [(k[b], q[a], i, base + BLOCKS + i) for i in range(by_key)]
            plain = [(q[a], k[b], i, base + BLOCKS - 1 - i) for i in range(by_query, BLOCKS)]
            plain += [(k[b], q[a], i, base + BLOCKS + i) for i in range(by_key, BLOCKS)]
            fold_count = len(folds_here)
            if fold_count:
                lower = folds.tile([P, MOST_FOLDS, HALF], F32, name="lower")
                larger = folds.tile([P, MOST_FOLDS, HALF], F32, name="larger")
            plain_count = len(plain)
            for i in range(MAXIMA):
                if chores:
                    for call in chores.pop(0):
                        call[0](*call[1:])
                if (i % 2 == 1 or not folds_here if n == PAIRS - 1 else -(-(i + 1) * plain_count // MAXIMA) > -(-i * plain_count // MAXIMA)):
                    plain_logits(*plain.pop(0))
                else:
                    side = fold_count - len(folds_here)
                    folded_logits(*folds_here.pop(0), (lower, larger, side, fold_count))
                if len(waiting) > LOOKAHEAD:
                    take_maximum()
        while waiting:
            take_maximum()
            if folded:
                take_folded_maxima()
        while folded:
            take_folded_maxima()

        sums = keep.tile([P, PAIRS], F32, name="sums")
        nc.vector.tensor_reduce(
            out=sums[:],
            in_=maxima[:].rearrange("p (n c) -> p n c", c=MAXIMA),
            axis=AXIS.X,
            op=ALU.add,
        )
        totals = banks.tile([P, PAIRS], F32, name="totals", tag="bank")
        nc.tensor.matmul(out=totals[:], lhsT=ones[:], rhs=sums[:], start=True, stop=True)
        result = keep.tile([P, PAIRS // STORE_RUN, 2 * STORE_RUN], F32, name="result")
        nc.vector.tensor_scalar(
            out=result[:, :, 0:STORE_RUN],
            in0=totals[:].rearrange("p (h c) -> p h c", c=STORE_RUN),
            scalar1=gain[:, 0:1],
            scalar2=1.0 / (2 * ROWS),
            op0=ALU.mult,
            op1=ALU.mult,
        )
        nc.sync.dma_start(
            out=out.rearrange("(o h a) b -> o h (a b)", o=1, h=PAIRS // STORE_RUN),
            in_=result[0:1, :, 0:STORE_RUN],
        )
